import numpy as np
import ml_dtypes


def mxq(x, axis, fmt="e4m3"):
    dtype, down = {"e4m3": (ml_dtypes.float8_e4m3fn, 7), "e5m2": (ml_dtypes.float8_e5m2, 14)}[fmt]
    v = np.moveaxis(np.asarray(x, np.float32).astype(ml_dtypes.bfloat16).astype(np.float64), axis, -1)
    blocks = v.reshape(v.shape[:-1] + (-1, 32))
    amax = np.abs(blocks).max(-1, keepdims=True)
    byte = np.maximum(np.where(amax > 0, np.frexp(amax)[1] - 1 + 127, 0) - down, 1)
    scale = np.exp2(byte - 127.0)
    codes = (blocks / scale).astype(np.float32).astype(dtype).astype(np.float64)
    return np.moveaxis((codes * scale).reshape(v.shape), -1, axis)


WIDE = False


def mx_kscale(k):
    if not WIDE:
        return np.ones(k)
    levels = np.array([10, -10, 5, -5, 0])
    if k % 512:
        return np.exp2(np.random.permutation(np.resize(levels, k // 32))).repeat(32)
    a = np.empty((k // 512, 16))
    for p in range(k // 512):
        a[p, :8] = np.random.permutation(np.resize(levels, 8))
        for g in range(8):
            far = levels[np.abs(levels - a[p, g]) >= 10]
            a[p, g + 8] = far[np.random.randint(len(far))]
    return np.exp2(a.ravel()).repeat(32)


BF16 = ml_dtypes.bfloat16


def bf(x):
    return np.asarray(x, np.float32).astype(BF16)


def f64(x):
    return np.asarray(x).astype(np.float64)


B, T, D, H, E, C = 2, 1024, 1024, 8, 1024, 512
HD = D // H
EPS = 1e-5


def setup_inputs():
    s = mx_kscale(D)
    fall = 0.35 / np.sqrt(1.0 + np.arange(T))
    return {"ret": bf(np.random.standard_normal((B, T, H, HD)) * fall[None, :, None, None]),
            "gamma": bf((1.0 + 0.1 * np.random.standard_normal(D)) * s),
            "beta": bf(0.1 * np.random.standard_normal(D) * s),
            "Wo": bf(np.random.standard_normal((D, E)) / np.sqrt(D) / s[:, None]),
            "bo": bf(0.1 * np.random.standard_normal(E))}


def reference(ret, gamma, beta, Wo, bo):
    r = f64(ret)
    mu = r.mean(-1, keepdims=True)
    var = r.var(-1, keepdims=True)
    z = (r - mu) / np.sqrt(var + EPS)
    y = z.reshape(B, T, D) * f64(gamma) + f64(beta)
    return (mxq(y, 2, "e4m3") @ mxq(f64(Wo), 0, "e4m3")) + f64(bo)

@@ -1,0 +1,229 @@
+from contextlib import ExitStack
+
+import concourse.mybir as mybir
+from concourse.masks import make_identity
+
+FLOPS = 2 * 2048 * 1024 * 1024
+
+BF16 = mybir.dt.bfloat16
+F32 = mybir.dt.float32
+U32 = mybir.dt.uint32
+U8 = mybir.dt.uint8
+FP8X4 = mybir.dt.float8_e4m3fn_x4
+ALU = mybir.AluOpType
+ACT = mybir.ActivationFunctionType
+
+P = 128
+D = 1024
+E = 1024
+H = 8
+PASSES = 2
+PACK = 4
+BANK = 512
+SLOTS = 16
+GS = 2
+NG = SLOTS // GS
+GT = GS * P
+U = GS * H
+EPS = 1e-5
+QLAG = 2
+LOW = [0, 1, 2, 3]
+HIGH = [4, 5, 6, 7]
+
+
+def tile_retentivenetwork_pb_kernel(tc, ret, gamma, beta, Wo, bo, out):
+    nc = tc.nc
+    ret_v = ret.rearrange("b (q j) h c -> (b q) j (h c)", j=SLOTS)
+    out_v = out.rearrange("b (q j) e -> (b q) j e", j=SLOTS)
+    wo_v = Wo.rearrange("(a p t) n -> p a t n", a=PASSES, t=PACK)
+
+    with ExitStack() as ctx:
+        const = ctx.enter_context(tc.tile_pool(name="const", bufs=1))
+        small = ctx.enter_context(tc.tile_pool(name="small", bufs=3))
+        zpool = ctx.enter_context(tc.tile_pool(name="zpool", bufs=2))
+        ppool = ctx.enter_context(tc.tile_pool(name="ppool", bufs=2))
+        gpool = ctx.enter_context(tc.tile_pool(name="gpool", bufs=2))
+        cpool = ctx.enter_context(tc.tile_pool(name="cpool", bufs=2))
+        opool = ctx.enter_context(tc.tile_pool(name="opool", bufs=3))
+        tpsum = ctx.enter_context(tc.psum_pool(name="tpsum", bufs=4))
+        apsum = ctx.enter_context(tc.psum_pool(name="apsum", bufs=4))
+        ctx.enter_context(tc.manual_schedule())
+
+        xs = []
+        for g in range(NG):
+            xg = const.tile([P, GS, D], BF16, name="x%d" % g)
+            xs.append(xg)
+        wraw = const.tile([P, PASSES * PACK, E], BF16, name="wraw")
+        bias_b = const.tile([P, E], BF16, name="bias_b")
+
+        def load_x(g):
+            nc.sync.dma_start(out=xs[g][:], in_=ret_v[:, g * GS:(g + 1) * GS, :])
+
+        def load_w(a):
+            nc.sync.dma_start(out=wraw[:, PACK * a:PACK * (a + 1), :], in_=wo_v[:, a, :, :])
+
+        gam = const.tile([P, PASSES, PACK], BF16, name="gam")
+        bet = const.tile([P, PASSES, PACK], BF16, name="bet")
+        one = const.tile([P, 1], F32, name="one")
+        nc.vector.memset(one[:], 1.0)
+        nc.scalar.dma_start(out=gam[:], in_=gamma.rearrange("(a p t) -> p a t", a=PASSES, t=PACK))
+        nc.scalar.dma_start(out=bet[:], in_=beta.rearrange("(a p t) -> p a t", a=PASSES, t=PACK))
+        for s in range(GS):
+            nc.sync.dma_start(out=xs[0][:, s, :], in_=ret_v[:, s, :])
+        load_x(1)
+        load_w(0)
+        load_x(2)
+        load_w(1)
+        for g in range(3, NG):
+            load_x(g)
+        nc.sync.dma_start(out=bias_b[:], in_=bo.partition_broadcast(P))
+        warm = const.tile([P, 1], F32, name="warm")
+        nc.scalar.activation(out=warm[:], in_=one[:], func=ACT.Abs_reciprocal_sqrt)
+
+        ident = const.tile([P, P], F32, name="ident")
+        make_identity(nc, ident[:])
+        gbT = const.tile([P, 2 * H], F32, name="gbT")
+        nc.gpsimd.tensor_copy(out=gbT[:, 0:H], in_=gam[:].rearrange("p a t -> p (a t)"))
+        nc.gpsimd.tensor_copy(out=gbT[:, H:2 * H], in_=bet[:].rearrange("p a t -> p (a t)"))
+
+        wgrp = const.tile([P, PASSES, E, PACK], BF16, name="wgrp", align_bytes=64)
+        wc = const.tile([P, PASSES, E], U32, name="wc", align_bytes=64)
+        ws = const.tile([P, PASSES, E], U8, name="ws", align_bytes=64)
+
+        def regroup_w(i):
+            a, half = divmod(i, 2)
+            cols = slice(half * BANK, (half + 1) * BANK)
+            nc.vector.tensor_copy(
+                out=wgrp[:, a, cols, :].rearrange("p (c i) t -> p c t i", i=4),
+                in_=wraw[:, PACK * a:PACK * (a + 1), cols].rearrange("p t (c i) -> p c t i", i=4),
+            )
+
+        def quantise_w(a):
+            nc.vector.quantize_mx(
+                out=wc[:, a, :].bitcast(FP8X4), scales=ws[:, a, :],
+                in_=wgrp[:, a, :, :].rearrange("p c t -> p (c t)"),
+            )
+
+        st, sums, rstd, nb, z, zt, yp, yg, yc, ys, acc, o = {}, {}, {}, {}, {}, {}, {}, {}, {}, {}, {}, {}
+
+        def measure(g):
+            st[g] = small.tile([P, U, 6], F32, name="st")
+            for s in range(GS):
+                for h in range(H):
+                    nc.vector.bn_stats(out=st[g][:, s * H + h, :], in_=xs[g][:, s, h * P:(h + 1) * P])
+
+        def stats_first(g):
+            sums[g] = small.tile([P, U, 3], F32, name="sums")
+            nc.vector.tensor_tensor(out=sums[g][:], in0=st[g][:, :, 0:3], in1=st[g][:, :, 3:6], op=ALU.add)
+            dif = small.tile([P, U, 1], F32, name="dif")
+            nc.vector.tensor_tensor(out=dif[:], in0=st[g][:, :, 1:2], in1=st[g][:, :, 4:5], op=ALU.subtract)
+            q32 = small.tile([P, U, 1], F32, name="q32")
+            nc.vector.scalar_tensor_tensor(out=q32[:], in0=dif[:], scalar=32.0, in1=dif[:], op0=ALU.mult, op1=ALU.mult)
+            w128 = small.tile([P, U, 1], F32, name="w128")
+            nc.vector.scalar_tensor_tensor(out=w128[:], in0=q32[:], scalar=P * EPS, in1=sums[g][:, :, 2:3], op0=ALU.add, op1=ALU.add)
+            rstd[g] = small.tile([P, U, 1], F32, name="rstd")
+            nc.scalar.activation(out=rstd[g][:], in_=w128[:], func=ACT.Abs_reciprocal_sqrt, scale=1.0 / P)
+
+        def stats_second(g):
+            nb[g] = small.tile([P, U, 1], F32, name="nb")
+            nc.vector.scalar_tensor_tensor(out=nb[g][:], in0=sums[g][:, :, 1:2], scalar=-0.5, in1=rstd[g][:], op0=ALU.mult, op1=ALU.mult)
+
+        def normalise(g):
+            z[g] = zpool.tile([P, GS, H, P], F32, name="z")
+            for h in range(H):
+                a, j = divmod(h, PACK)
+                for s in range(GS):
+                    u = s * H + h
+                    nc.scalar.activation(
+                        out=z[g][:, s, PACK * a:PACK * (a + 1), 32 * j:32 * (j + 1)],
+                        in_=xs[g][:, s, h * P:(h + 1) * P].rearrange("p (i t) -> p t i", t=PACK),
+                        func=ACT.Identity, bias=nb[g][:, u, :], scale=rstd[g][:, u, :],
+                    )
+
+        def turn(g, heads):
+            for h in heads:
+                zt[(g, h)] = tpsum.tile([P, BANK], F32, tag="zt", name="zt")
+                for s in range(GS):
+                    nc.tensor.transpose(out=zt[(g, h)][:, s * P:(s + 1) * P], in_=z[g][:, s, h, :], identity=ident[:])
+
+        def leave_psum(g, heads):
+            if heads[0] == 0:
+                yp[g] = ppool.tile([P, H, GT], BF16, name="yp")
+            for h in heads:
+                nc.scalar.activation(
+                    out=yp[g][:, h, :], in_=zt[(g, h)][:, 0:GT], func=ACT.Identity,
+                    bias=gbT[:, H + h:H + h + 1], scale=gbT[:, h:h + 1],
+                )
+
+        def regroup_y(g, go):
+            yg[g] = gpool.tile([P, PASSES, GT, PACK], BF16, name="yg", align_bytes=64)
+            for a in range(PASSES):
+                nc.gpsimd.tensor_scalar(
+                    out=yg[g][:, a, :, :], in0=yp[g][:, PACK * a:PACK * (a + 1), :].rearrange("p t c -> p c t"),
+                    scalar1=go[:, 0:1], scalar2=0.0, op0=ALU.mult, op1=ALU.add,
+                )
+
+        def quantise_y(g):
+            yc[g] = cpool.tile([P, PASSES * GT], U32, name="yc", align_bytes=64)
+            ys[g] = cpool.tile([P, PASSES * GT], U8, name="ys", align_bytes=64)
+            nc.vector.quantize_mx(out=yc[g][:].bitcast(FP8X4), scales=ys[g][:], in_=yg[g][:].rearrange("p a c t -> p (a c t)"))
+
+        def project(g):
+            for s in range(GS):
+                for n in range(E // BANK):
+                    acc[(g, s, n)] = apsum.tile([P, BANK], F32, tag="acc", name="acc")
+                    for a in range(PASSES):
+                        m_cols = slice(a * GT + s * P, a * GT + (s + 1) * P)
+                        n_cols = slice(n * BANK, (n + 1) * BANK)
+                        nc.tensor.matmul_mx(
+                            out=acc[(g, s, n)][:],
+                            lhsT=yc[g][:, m_cols].bitcast(FP8X4), lhsT_scale=ys[g][:, m_cols],
+                            rhs=wc[:, a, n_cols].bitcast(FP8X4), rhs_scale=ws[:, a, n_cols],
+                            start=(a == 0), stop=(a == PASSES - 1),
+                        )
+
+        def finish(g, banks):
+            if banks[0] == 0:
+                o[g] = opool.tile([P, GS, E], F32, name="o")
+            for i in banks:
+                s, n = divmod(i, 2)
+                nc.vector.tensor_tensor(out=o[g][:, s, n * BANK:(n + 1) * BANK], in0=acc[(g, s, n)][:], in1=bias_b[:, n * BANK:(n + 1) * BANK], op=ALU.add)
+                if n == 1 and g == NG - 1:
+                    nc.sync.dma_start(out=out_v[:, g * GS + s, :], in_=o[g][:, s, :])
+            if banks[-1] == 3 and g < NG - 1:
+                nc.sync.dma_start(out=out_v[:, g * GS:(g + 1) * GS, :], in_=o[g][:])
+
+        def live(g):
+            return 0 <= g < NG
+
+        for k in range(NG + QLAG + 1):
+            if live(k):
+                measure(k)
+            if k in (1, 2):
+                regroup_w(2 * k - 2)
+            if live(k - QLAG - 1):
+                finish(k - QLAG - 1, [0, 1, 2])
+            if live(k):
+                stats_first(k)
+            if live(k - 1):
+                leave_psum(k - 1, HIGH)
+            if k in (1, 2):
+                regroup_w(2 * k - 1)
+            if live(k - QLAG - 1):
+                finish(k - QLAG - 1, [3])
+            if k in (1, 2):
+                quantise_w(k - 1)
+            if live(k - QLAG):
+                quantise_y(k - QLAG)
+                project(k - QLAG)
+            if live(k):
+                stats_second(k)
+            if live(k - 1):
+                go = small.tile([P, 1], F32, name="go")
+                nc.vector.memset(go[:], 1.0)
+                regroup_y(k - 1, go)
+            if live(k):
+                normalise(k)
+                turn(k, LOW)
+                leave_psum(k, LOW)
+                turn(k, HIGH)

@@ -104,29 +104,25 @@ def tile_retentivenetwork_pb_kernel(tc, ret, gamma, beta, Wo, bo, out):
                 in_=wgrp[:, a, :, :].rearrange("p c t -> p (c t)"),
             )
 
-        st, sums, rstd, nb, z, zt, yp, yg, yc, ys, acc, o = {}, {}, {}, {}, {}, {}, {}, {}, {}, {}, {}, {}
+        st, rstd, nb, z, zt, yp, yg, yc, ys, acc, o = {}, {}, {}, {}, {}, {}, {}, {}, {}, {}, {}
 
         def measure(g):
-            st[g] = small.tile([P, U, 6], F32, name="st")
+            st[g] = small.tile([P, U, 3], F32, name="st")
             for s in range(GS):
-                for h in range(H):
-                    nc.vector.bn_stats(out=st[g][:, s * H + h, :], in_=xs[g][:, s, h * P:(h + 1) * P])
+                for h in range(0, H, 2):
+                    u = s * H + h
+                    nc.vector.bn_stats(
+                        out=st[g][:, u:u + 2, :].rearrange("p u v -> p (u v)"),
+                        in_=xs[g][:, s, h * P:(h + 2) * P].rearrange("p (e c) -> p c e", e=2),
+                    )
 
         def stats_first(g):
-            sums[g] = small.tile([P, U, 3], F32, name="sums")
-            nc.vector.tensor_tensor(out=sums[g][:], in0=st[g][:, :, 0:3], in1=st[g][:, :, 3:6], op=ALU.add)
-            dif = small.tile([P, U, 1], F32, name="dif")
-            nc.vector.tensor_tensor(out=dif[:], in0=st[g][:, :, 1:2], in1=st[g][:, :, 4:5], op=ALU.subtract)
-            q32 = small.tile([P, U, 1], F32, name="q32")
-            nc.vector.scalar_tensor_tensor(out=q32[:], in0=dif[:], scalar=32.0, in1=dif[:], op0=ALU.mult, op1=ALU.mult)
-            w128 = small.tile([P, U, 1], F32, name="w128")
-            nc.vector.scalar_tensor_tensor(out=w128[:], in0=q32[:], scalar=P * EPS, in1=sums[g][:, :, 2:3], op0=ALU.add, op1=ALU.add)
             rstd[g] = small.tile([P, U, 1], F32, name="rstd")
-            nc.scalar.activation(out=rstd[g][:], in_=w128[:], func=ACT.Abs_reciprocal_sqrt, scale=1.0 / P)
+            nc.scalar.activation(out=rstd[g][:], in_=st[g][:, :, 2:3], func=ACT.Abs_reciprocal_sqrt, scale=1.0 / P, bias=EPS)
 
         def stats_second(g):
             nb[g] = small.tile([P, U, 1], F32, name="nb")
-            nc.vector.scalar_tensor_tensor(out=nb[g][:], in0=sums[g][:, :, 1:2], scalar=-0.5, in1=rstd[g][:], op0=ALU.mult, op1=ALU.mult)
+            nc.vector.scalar_tensor_tensor(out=nb[g][:], in0=st[g][:, :, 1:2], scalar=-1.0, in1=rstd[g][:], op0=ALU.mult, op1=ALU.mult)
 
         def normalise(g):
             z[g] = zpool.tile([P, GS, H, P], F32, name="z")

@@ -21,14 +21,9 @@ PASSES = 2
 PACK = 4
 BANK = 512
 SLOTS = 16
-GS = 2
-NG = SLOTS // GS
-GT = GS * P
-U = GS * H
+SIZES = [1, 1, 2, 2, 2, 2, 2, 2, 1, 1]
+NG = len(SIZES)
 EPS = 1e-5
-QLAG = 2
-LOW = [0, 1, 2, 3]
-HIGH = [4, 5, 6, 7]
 
 
 def tile_retentivenetwork_pb_kernel(tc, ret, gamma, beta, Wo, bo, out):
@@ -36,10 +31,11 @@ def tile_retentivenetwork_pb_kernel(tc, ret, gamma, beta, Wo, bo, out):
     ret_v = ret.rearrange("b (q j) h c -> (b q) j (h c)", j=SLOTS)
     out_v = out.rearrange("b (q j) e -> (b q) j e", j=SLOTS)
     wo_v = Wo.rearrange("(a p t) n -> p a t n", a=PASSES, t=PACK)
+    first = [sum(SIZES[:g]) for g in range(NG)]
 
     with ExitStack() as ctx:
         const = ctx.enter_context(tc.tile_pool(name="const", bufs=1))
-        small = ctx.enter_context(tc.tile_pool(name="small", bufs=3))
+        small = ctx.enter_context(tc.tile_pool(name="small", bufs=NG))
         zpool = ctx.enter_context(tc.tile_pool(name="zpool", bufs=2))
         ppool = ctx.enter_context(tc.tile_pool(name="ppool", bufs=2))
         gpool = ctx.enter_context(tc.tile_pool(name="gpool", bufs=2))
@@ -51,16 +47,17 @@ def tile_retentivenetwork_pb_kernel(tc, ret, gamma, beta, Wo, bo, out):
 
         xs = []
         for g in range(NG):
-            xg = const.tile([P, GS, D], BF16, name="x%d" % g)
+            xg = const.tile([P, SIZES[g], D], BF16, name="x%d" % g)
             xs.append(xg)
         wraw = const.tile([P, PASSES * PACK, E], BF16, name="wraw")
         bias_b = const.tile([P, E], BF16, name="bias_b")
 
         def load_x(g):
-            nc.sync.dma_start(out=xs[g][:], in_=ret_v[:, g * GS:(g + 1) * GS, :])
+            nc.sync.dma_start(out=xs[g][:], in_=ret_v[:, first[g]:first[g] + SIZES[g], :])
 
-        def load_w(a):
-            nc.sync.dma_start(out=wraw[:, PACK * a:PACK * (a + 1), :], in_=wo_v[:, a, :, :])
+        def load_w(a, half):
+            cols = slice(half * BANK, (half + 1) * BANK)
+            nc.sync.dma_start(out=wraw[:, PACK * a:PACK * (a + 1), cols], in_=wo_v[:, a, :, cols])
 
         gam = const.tile([P, PASSES, PACK], BF16, name="gam")
         bet = const.tile([P, PASSES, PACK], BF16, name="bet")
@@ -68,13 +65,15 @@ def tile_retentivenetwork_pb_kernel(tc, ret, gamma, beta, Wo, bo, out):
         nc.vector.memset(one[:], 1.0)
         nc.scalar.dma_start(out=gam[:], in_=gamma.rearrange("(a p t) -> p a t", a=PASSES, t=PACK))
         nc.scalar.dma_start(out=bet[:], in_=beta.rearrange("(a p t) -> p a t", a=PASSES, t=PACK))
-        for s in range(GS):
-            nc.sync.dma_start(out=xs[0][:, s, :], in_=ret_v[:, s, :])
+        load_x(0)
         load_x(1)
-        load_w(0)
+        load_w(1, 0)
         load_x(2)
-        load_w(1)
-        for g in range(3, NG):
+        load_w(1, 1)
+        load_w(0, 0)
+        load_x(3)
+        load_w(0, 1)
+        for g in range(4, NG):
             load_x(g)
         nc.sync.dma_start(out=bias_b[:], in_=bo.partition_broadcast(P))
         warm = const.tile([P, 1], F32, name="warm")
@@ -90,13 +89,22 @@ def tile_retentivenetwork_pb_kernel(tc, ret, gamma, beta, Wo, bo, out):
         wc = const.tile([P, PASSES, E], U32, name="wc", align_bytes=64)
         ws = const.tile([P, PASSES, E], U8, name="ws", align_bytes=64)
 
-        def regroup_w(i):
-            a, half = divmod(i, 2)
+        def w_views(a, half):
             cols = slice(half * BANK, (half + 1) * BANK)
-            nc.vector.tensor_copy(
-                out=wgrp[:, a, cols, :].rearrange("p (c i) t -> p c t i", i=4),
-                in_=wraw[:, PACK * a:PACK * (a + 1), cols].rearrange("p t (c i) -> p c t i", i=4),
-            )
+            return (wgrp[:, a, cols, :].rearrange("p (c i) t -> p c t i", i=4),
+                    wraw[:, PACK * a:PACK * (a + 1), cols].rearrange("p t (c i) -> p c t i", i=4))
+
+        def regroup_w_vector(a, half):
+            dst, src = w_views(a, half)
+            nc.vector.tensor_copy(out=dst, in_=src)
+
+        def regroup_w_gpsimd(a, half):
+            for quarter in (2 * half, 2 * half + 1):
+                cols = slice(quarter * 256, (quarter + 1) * 256)
+                nc.gpsimd.tensor_scalar(
+                    out=wgrp[:, a, cols, :], in0=wraw[:, PACK * a:PACK * (a + 1), cols].rearrange("p t c -> p c t"),
+                    scalar1=1.0, scalar2=0.0, op0=ALU.mult, op1=ALU.add,
+                )
 
         def quantise_w(a):
             nc.vector.quantize_mx(
@@ -104,11 +112,11 @@ def tile_retentivenetwork_pb_kernel(tc, ret, gamma, beta, Wo, bo, out):
                 in_=wgrp[:, a, :, :].rearrange("p c t -> p (c t)"),
             )
 
-        st, rstd, nb, z, zt, yp, yg, yc, ys, acc, o = {}, {}, {}, {}, {}, {}, {}, {}, {}, {}, {}
+        st, rstd, nb, z, zt, yp, yg, yc, ys, acc = {}, {}, {}, {}, {}, {}, {}, {}, {}, {}
 
         def measure(g):
-            st[g] = small.tile([P, U, 3], F32, name="st")
-            for s in range(GS):
+            st[g] = small.tile([P, SIZES[g] * H, 3], F32, name="st")
+            for s in range(SIZES[g]):
                 for h in range(0, H, 2):
                     u = s * H + h
                     nc.vector.bn_stats(
@@ -116,19 +124,26 @@ def tile_retentivenetwork_pb_kernel(tc, ret, gamma, beta, Wo, bo, out):
                         in_=xs[g][:, s, h * P:(h + 2) * P].rearrange("p (e c) -> p c e", e=2),
                     )
 
-        def stats_first(g):
-            rstd[g] = small.tile([P, U, 1], F32, name="rstd")
+        def root(g):
+            rstd[g] = small.tile([P, SIZES[g] * H, 1], F32, name="rstd")
             nc.scalar.activation(out=rstd[g][:], in_=st[g][:, :, 2:3], func=ACT.Abs_reciprocal_sqrt, scale=1.0 / P, bias=EPS)
 
-        def stats_second(g):
-            nb[g] = small.tile([P, U, 1], F32, name="nb")
+        def shift(g):
+            nb[g] = small.tile([P, SIZES[g] * H, 1], F32, name="nb")
             nc.vector.scalar_tensor_tensor(out=nb[g][:], in0=st[g][:, :, 1:2], scalar=-1.0, in1=rstd[g][:], op0=ALU.mult, op1=ALU.mult)
 
-        def normalise(g):
-            z[g] = zpool.tile([P, GS, H, P], F32, name="z")
-            for h in range(H):
-                a, j = divmod(h, PACK)
-                for s in range(GS):
+        def shift_gpsimd(g):
+            nb[g] = small.tile([P, SIZES[g] * H, 1], F32, name="nb")
+            negm = small.tile([P, SIZES[g] * H, 1], F32, name="negm")
+            nc.gpsimd.tensor_scalar(out=negm[:], in0=st[g][:, :, 1:2], scalar1=-1.0, scalar2=0.0, op0=ALU.mult, op1=ALU.add)
+            nc.gpsimd.tensor_tensor(out=nb[g][:], in0=negm[:], in1=rstd[g][:], op=ALU.mult)
+
+        def normalise(g, a):
+            if a == 0:
+                z[g] = zpool.tile([P, SIZES[g], H, P], F32, name="z")
+            for j in range(PACK):
+                h = PACK * a + j
+                for s in range(SIZES[g]):
                     u = s * H + h
                     nc.scalar.activation(
                         out=z[g][:, s, PACK * a:PACK * (a + 1), 32 * j:32 * (j + 1)],
@@ -136,40 +151,43 @@ def tile_retentivenetwork_pb_kernel(tc, ret, gamma, beta, Wo, bo, out):
                         func=ACT.Identity, bias=nb[g][:, u, :], scale=rstd[g][:, u, :],
                     )
 
-        def turn(g, heads):
-            for h in heads:
-                zt[(g, h)] = tpsum.tile([P, BANK], F32, tag="zt", name="zt")
-                for s in range(GS):
-                    nc.tensor.transpose(out=zt[(g, h)][:, s * P:(s + 1) * P], in_=z[g][:, s, h, :], identity=ident[:])
+        def turn(g, a):
+            for v in range(PACK * a, PACK * (a + 1)):
+                zt[(g, v)] = tpsum.tile([P, BANK], F32, tag="zt", name="zt")
+                for s in range(SIZES[g]):
+                    nc.tensor.transpose(out=zt[(g, v)][:, s * P:(s + 1) * P], in_=z[g][:, s, v, :], identity=ident[:])
 
-        def leave_psum(g, heads):
-            if heads[0] == 0:
-                yp[g] = ppool.tile([P, H, GT], BF16, name="yp")
-            for h in heads:
+        def leave_psum(g, a):
+            yp[(g, a)] = ppool.tile([P, PACK, SIZES[g] * P], BF16, name="yp%d" % a)
+            for t in range(PACK):
+                v = PACK * a + t
                 nc.scalar.activation(
-                    out=yp[g][:, h, :], in_=zt[(g, h)][:, 0:GT], func=ACT.Identity,
-                    bias=gbT[:, H + h:H + h + 1], scale=gbT[:, h:h + 1],
+                    out=yp[(g, a)][:, t, :], in_=zt[(g, v)][:, 0:SIZES[g] * P], func=ACT.Identity,
+                    bias=gbT[:, H + v:H + v + 1], scale=gbT[:, v:v + 1],
                 )
 
-        def regroup_y(g, go):
-            yg[g] = gpool.tile([P, PASSES, GT, PACK], BF16, name="yg", align_bytes=64)
-            for a in range(PASSES):
-                nc.gpsimd.tensor_scalar(
-                    out=yg[g][:, a, :, :], in0=yp[g][:, PACK * a:PACK * (a + 1), :].rearrange("p t c -> p c t"),
-                    scalar1=go[:, 0:1], scalar2=0.0, op0=ALU.mult, op1=ALU.add,
-                )
+        def regroup_y(g, a, go):
+            if a == 0:
+                yg[g] = gpool.tile([P, PASSES, SIZES[g] * P, PACK], BF16, name="yg", align_bytes=64)
+            src = yp[(g, a)][:].rearrange("p t c -> p c t")
+            if g == NG - 1:
+                nc.vector.tensor_copy(out=yg[g][:, a, :, :], in_=src)
+            else:
+                nc.gpsimd.tensor_scalar(out=yg[g][:, a, :, :], in0=src, scalar1=go[:, 0:1], scalar2=0.0, op0=ALU.mult, op1=ALU.add)
 
         def quantise_y(g):
-            yc[g] = cpool.tile([P, PASSES * GT], U32, name="yc", align_bytes=64)
-            ys[g] = cpool.tile([P, PASSES * GT], U8, name="ys", align_bytes=64)
+            words = PASSES * SIZES[g] * P
+            yc[g] = cpool.tile([P, words], U32, name="yc", align_bytes=64)
+            ys[g] = cpool.tile([P, words], U8, name="ys", align_bytes=64)
             nc.vector.quantize_mx(out=yc[g][:].bitcast(FP8X4), scales=ys[g][:], in_=yg[g][:].rearrange("p a c t -> p (a c t)"))
 
         def project(g):
-            for s in range(GS):
+            for s in range(SIZES[g]):
                 for n in range(E // BANK):
                     acc[(g, s, n)] = apsum.tile([P, BANK], F32, tag="acc", name="acc")
                     for a in range(PASSES):
-                        m_cols = slice(a * GT + s * P, a * GT + (s + 1) * P)
+                        m0 = (a * SIZES[g] + s) * P
+                        m_cols = slice(m0, m0 + P)
                         n_cols = slice(n * BANK, (n + 1) * BANK)
                         nc.tensor.matmul_mx(
                             out=acc[(g, s, n)][:],
@@ -178,48 +196,62 @@ def tile_retentivenetwork_pb_kernel(tc, ret, gamma, beta, Wo, bo, out):
                             start=(a == 0), stop=(a == PASSES - 1),
                         )
 
-        def finish(g, banks):
-            if banks[0] == 0:
-                o[g] = opool.tile([P, GS, E], F32, name="o")
-            for i in banks:
-                s, n = divmod(i, 2)
-                nc.vector.tensor_tensor(out=o[g][:, s, n * BANK:(n + 1) * BANK], in0=acc[(g, s, n)][:], in1=bias_b[:, n * BANK:(n + 1) * BANK], op=ALU.add)
-                if n == 1 and g == NG - 1:
-                    nc.sync.dma_start(out=out_v[:, g * GS + s, :], in_=o[g][:, s, :])
-            if banks[-1] == 3 and g < NG - 1:
-                nc.sync.dma_start(out=out_v[:, g * GS:(g + 1) * GS, :], in_=o[g][:])
+        def finish(g):
+            o = opool.tile([P, SIZES[g], E], F32, name="o")
+            for s in range(SIZES[g]):
+                for n in range(E // BANK):
+                    n_cols = slice(n * BANK, (n + 1) * BANK)
+                    nc.vector.tensor_tensor(out=o[:, s, n_cols], in0=acc[(g, s, n)][:], in1=bias_b[:, n_cols], op=ALU.add)
+            nc.sync.dma_start(out=out_v[:, first[g]:first[g] + SIZES[g], :], in_=o[:])
 
         def live(g):
             return 0 <= g < NG
 
-        for k in range(NG + QLAG + 1):
+        go = one
+        for k in range(-2, NG + 2):
+            due = [0, 1] if k == 3 else [k - 2] if 3 < k else []
+            if k == -1:
+                root(0)
+                shift_gpsimd(0)
             if live(k):
-                measure(k)
-            if k in (1, 2):
-                regroup_w(2 * k - 2)
-            if live(k - QLAG - 1):
-                finish(k - QLAG - 1, [0, 1, 2])
-            if live(k):
-                stats_first(k)
+                normalise(k, 0)
             if live(k - 1):
-                leave_psum(k - 1, HIGH)
-            if k in (1, 2):
-                regroup_w(2 * k - 1)
-            if live(k - QLAG - 1):
-                finish(k - QLAG - 1, [3])
-            if k in (1, 2):
-                quantise_w(k - 1)
-            if live(k - QLAG):
-                quantise_y(k - QLAG)
-                project(k - QLAG)
+                leave_psum(k - 1, 1)
+            if k >= 0 and live(k + 1):
+                root(k + 1)
+            if k >= 1 and live(k + 1):
+                shift(k + 1)
+            if live(k + 2):
+                measure(k + 2)
+            if k == -1:
+                regroup_w_vector(1, 0)
+            if k == 1:
+                regroup_w_vector(0, 0)
+            if k == 2:
+                quantise_w(1)
+                quantise_w(0)
             if live(k):
-                stats_second(k)
+                turn(k, 0)
+            for g in due:
+                project(g)
+            if live(k):
+                normalise(k, 1)
+                leave_psum(k, 0)
+                turn(k, 1)
             if live(k - 1):
+                regroup_y(k - 1, 0, go)
+                regroup_y(k - 1, 1, go)
+            if k == 0:
+                shift_gpsimd(1)
+                regroup_w_gpsimd(1, 1)
+            if k == 1:
+                regroup_w_gpsimd(0, 1)
+            if k == NG:
+                quantise_y(k - 1)
+            for g in due:
+                finish(g)
+            if live(k - 1) and k < NG:
+                quantise_y(k - 1)
+            if 3 <= k < NG - 1:
                 go = small.tile([P, 1], F32, name="go")
                 nc.vector.memset(go[:], 1.0)
-                regroup_y(k - 1, go)
-            if live(k):
-                normalise(k)
-                turn(k, LOW)
-                leave_psum(k, LOW)
-                turn(k, HIGH)

@@ -24,6 +24,7 @@ SLOTS = 16
 SIZES = [1, 1, 2, 2, 2, 2, 2, 2, 1, 1]
 NG = len(SIZES)
 EPS = 1e-5
+LATE = 2
 
 
 def tile_retentivenetwork_pb_kernel(tc, ret, gamma, beta, Wo, bo, out):
@@ -55,9 +56,8 @@ def tile_retentivenetwork_pb_kernel(tc, ret, gamma, beta, Wo, bo, out):
         def load_x(g):
             nc.sync.dma_start(out=xs[g][:], in_=ret_v[:, first[g]:first[g] + SIZES[g], :])
 
-        def load_w(a, half):
-            cols = slice(half * BANK, (half + 1) * BANK)
-            nc.sync.dma_start(out=wraw[:, PACK * a:PACK * (a + 1), cols], in_=wo_v[:, a, :, cols])
+        def load_w(a):
+            nc.sync.dma_start(out=wraw[:, PACK * a:PACK * (a + 1), :], in_=wo_v[:, a, :, :])
 
         gam = const.tile([P, PASSES, PACK], BF16, name="gam")
         bet = const.tile([P, PASSES, PACK], BF16, name="bet")
@@ -67,12 +67,10 @@ def tile_retentivenetwork_pb_kernel(tc, ret, gamma, beta, Wo, bo, out):
         nc.scalar.dma_start(out=bet[:], in_=beta.rearrange("(a p t) -> p a t", a=PASSES, t=PACK))
         load_x(0)
         load_x(1)
-        load_w(1, 0)
         load_x(2)
-        load_w(1, 1)
-        load_w(0, 0)
+        load_w(1)
         load_x(3)
-        load_w(0, 1)
+        load_w(0)
         for g in range(4, NG):
             load_x(g)
         nc.sync.dma_start(out=bias_b[:], in_=bo.partition_broadcast(P))
@@ -98,13 +96,9 @@ def tile_retentivenetwork_pb_kernel(tc, ret, gamma, beta, Wo, bo, out):
             dst, src = w_views(a, half)
             nc.vector.tensor_copy(out=dst, in_=src)
 
-        def regroup_w_gpsimd(a, half):
-            for quarter in (2 * half, 2 * half + 1):
-                cols = slice(quarter * 256, (quarter + 1) * 256)
-                nc.gpsimd.tensor_scalar(
-                    out=wgrp[:, a, cols, :], in0=wraw[:, PACK * a:PACK * (a + 1), cols].rearrange("p t c -> p c t"),
-                    scalar1=1.0, scalar2=0.0, op0=ALU.mult, op1=ALU.add,
-                )
+        def regroup_w_scalar(a, half):
+            dst, src = w_views(a, half)
+            nc.scalar.copy(out=dst, in_=src)
 
         def quantise_w(a):
             nc.vector.quantize_mx(
@@ -131,12 +125,6 @@ def tile_retentivenetwork_pb_kernel(tc, ret, gamma, beta, Wo, bo, out):
         def shift(g):
             nb[g] = small.tile([P, SIZES[g] * H, 1], F32, name="nb")
             nc.vector.scalar_tensor_tensor(out=nb[g][:], in0=st[g][:, :, 1:2], scalar=-1.0, in1=rstd[g][:], op0=ALU.mult, op1=ALU.mult)
-
-        def shift_gpsimd(g):
-            nb[g] = small.tile([P, SIZES[g] * H, 1], F32, name="nb")
-            negm = small.tile([P, SIZES[g] * H, 1], F32, name="negm")
-            nc.gpsimd.tensor_scalar(out=negm[:], in0=st[g][:, :, 1:2], scalar1=-1.0, scalar2=0.0, op0=ALU.mult, op1=ALU.add)
-            nc.gpsimd.tensor_tensor(out=nb[g][:], in0=negm[:], in1=rstd[g][:], op=ALU.mult)
 
         def normalise(g, a):
             if a == 0:
@@ -170,7 +158,7 @@ def tile_retentivenetwork_pb_kernel(tc, ret, gamma, beta, Wo, bo, out):
             if a == 0:
                 yg[g] = gpool.tile([P, PASSES, SIZES[g] * P, PACK], BF16, name="yg", align_bytes=64)
             src = yp[(g, a)][:].rearrange("p t c -> p c t")
-            if g == NG - 1:
+            if g >= NG - LATE:
                 nc.vector.tensor_copy(out=yg[g][:, a, :, :], in_=src)
             else:
                 nc.gpsimd.tensor_scalar(out=yg[g][:, a, :, :], in0=src, scalar1=go[:, 0:1], scalar2=0.0, op0=ALU.mult, op1=ALU.add)
@@ -212,46 +200,43 @@ def tile_retentivenetwork_pb_kernel(tc, ret, gamma, beta, Wo, bo, out):
             due = [0, 1] if k == 3 else [k - 2] if 3 < k else []
             if k == -1:
                 root(0)
-                shift_gpsimd(0)
+                shift(0)
             if live(k):
                 normalise(k, 0)
-            if live(k - 1):
-                leave_psum(k - 1, 1)
             if k >= 0 and live(k + 1):
                 root(k + 1)
-            if k >= 1 and live(k + 1):
                 shift(k + 1)
             if live(k + 2):
                 measure(k + 2)
-            if k == -1:
+            if k == 0:
                 regroup_w_vector(1, 0)
             if k == 1:
                 regroup_w_vector(0, 0)
-            if k == 2:
-                quantise_w(1)
-                quantise_w(0)
+                regroup_w_vector(0, 1)
             if live(k):
                 turn(k, 0)
+            if live(k - 1):
+                leave_psum(k - 1, 1)
             for g in due:
                 project(g)
             if live(k):
                 normalise(k, 1)
                 leave_psum(k, 0)
                 turn(k, 1)
+            if k == 1:
+                regroup_w_scalar(1, 1)
+            if k == 2:
+                quantise_w(1)
+                quantise_w(0)
             if live(k - 1):
                 regroup_y(k - 1, 0, go)
                 regroup_y(k - 1, 1, go)
-            if k == 0:
-                shift_gpsimd(1)
-                regroup_w_gpsimd(1, 1)
-            if k == 1:
-                regroup_w_gpsimd(0, 1)
-            if k == NG:
+            if k >= NG and live(k - 1):
                 quantise_y(k - 1)
             for g in due:
                 finish(g)
             if live(k - 1) and k < NG:
                 quantise_y(k - 1)
-            if 3 <= k < NG - 1:
+            if 2 <= k < NG - 1:
                 go = small.tile([P, 1], F32, name="go")
                 nc.vector.memset(go[:], 1.0)

@@ -65,7 +65,9 @@ def tile_retentivenetwork_pb_kernel(tc, ret, gamma, beta, Wo, bo, out):
         nc.vector.memset(one[:], 1.0)
         nc.scalar.dma_start(out=gam[:], in_=gamma.rearrange("(a p t) -> p a t", a=PASSES, t=PACK))
         nc.scalar.dma_start(out=bet[:], in_=beta.rearrange("(a p t) -> p a t", a=PASSES, t=PACK))
-        load_x(0)
+        for h in range(PASSES):
+            half = slice(h * BANK, (h + 1) * BANK)
+            nc.sync.dma_start(out=xs[0][:, 0, half], in_=ret_v[:, 0, half])
         load_x(1)
         load_x(2)
         load_w(1)
@@ -140,14 +142,16 @@ def tile_retentivenetwork_pb_kernel(tc, ret, gamma, beta, Wo, bo, out):
                     )
 
         def turn(g, a):
-            for v in range(PACK * a, PACK * (a + 1)):
-                zt[(g, v)] = tpsum.tile([P, BANK], F32, tag="zt", name="zt")
-                for s in range(SIZES[g]):
-                    nc.tensor.transpose(out=zt[(g, v)][:, s * P:(s + 1) * P], in_=z[g][:, s, v, :], identity=ident[:])
+            for v in range(PACK * a, PACK * (a + 1), 2):
+                pair = tpsum.tile([P, 2, BANK // 2], F32, tag="zt", name="zt")
+                for i in range(2):
+                    zt[(g, v + i)] = pair[:, i, :]
+                    for s in range(SIZES[g]):
+                        nc.tensor.transpose(out=pair[:, i, s * P:(s + 1) * P], in_=z[g][:, s, v + i, :], identity=ident[:])
 
         def leave_psum(g, a):
             yp[(g, a)] = ppool.tile([P, PACK, SIZES[g] * P], BF16, name="yp%d" % a)
-            for t in range(PACK):
+            for t in (1, 0, 3, 2):
                 v = PACK * a + t
                 nc.scalar.activation(
                     out=yp[(g, a)][:, t, :], in_=zt[(g, v)][:, 0:SIZES[g] * P], func=ACT.Identity,
@@ -190,7 +194,10 @@ def tile_retentivenetwork_pb_kernel(tc, ret, gamma, beta, Wo, bo, out):
                 for n in range(E // BANK):
                     n_cols = slice(n * BANK, (n + 1) * BANK)
                     nc.vector.tensor_tensor(out=o[:, s, n_cols], in0=acc[(g, s, n)][:], in1=bias_b[:, n_cols], op=ALU.add)
-            nc.sync.dma_start(out=out_v[:, first[g]:first[g] + SIZES[g], :], in_=o[:])
+                    if g == NG - 1:
+                        nc.sync.dma_start(out=out_v[:, first[g] + s, n_cols], in_=o[:, s, n_cols])
+            if g < NG - 1:
+                nc.sync.dma_start(out=out_v[:, first[g]:first[g] + SIZES[g], :], in_=o[:])
 
         def live(g):
             return 0 <= g < NG

@@ -110,11 +110,14 @@ def tile_retentivenetwork_pb_kernel(tc, ret, gamma, beta, Wo, bo, out):
 
         st, rstd, nb, z, zt, yp, yg, yc, ys, acc = {}, {}, {}, {}, {}, {}, {}, {}, {}, {}
 
-        def measure(g):
-            st[g] = small.tile([P, SIZES[g] * H, 3], F32, name="st")
+        def measure(g, part=2):
+            if part != 1:
+                st[g] = small.tile([P, SIZES[g] * H, 3], F32, name="st")
             for s in range(SIZES[g]):
                 for h in range(0, H, 2):
                     u = s * H + h
+                    if part < 2 and u * 2 // (SIZES[g] * H) != part:
+                        continue
                     nc.vector.bn_stats(
                         out=st[g][:, u:u + 2, :].rearrange("p u v -> p (u v)"),
                         in_=xs[g][:, s, h * P:(h + 2) * P].rearrange("p (e c) -> p c e", e=2),
@@ -207,14 +210,19 @@ def tile_retentivenetwork_pb_kernel(tc, ret, gamma, beta, Wo, bo, out):
             due = [0, 1] if k == 3 else [k - 2] if 3 < k else []
             if k == -1:
                 root(0)
-                shift(0)
             if live(k):
                 normalise(k, 0)
             if k >= 0 and live(k + 1):
                 root(k + 1)
+            if -1 <= k < 2:
+                measure(k + 2, 0)
                 shift(k + 1)
-            if live(k + 2):
-                measure(k + 2)
+                measure(k + 2, 1)
+            else:
+                if live(k + 1) and k >= 0:
+                    shift(k + 1)
+                if live(k + 2):
+                    measure(k + 2)
             if k == 0:
                 regroup_w_vector(1, 0)
             if k == 1:

@@ -180,6 +180,8 @@ def tile_retentivenetwork_pb_kernel(tc, ret, gamma, beta, Wo, bo, out):
             for s in range(SIZES[g]):
                 for n in range(E // BANK):
                     acc[(g, s, n)] = apsum.tile([P, BANK], F32, tag="acc", name="acc")
+                    if g >= 5 and s == 0 and n == 0:
+                        nc.tensor.matmul(out=acc[(g, s, n)][:], lhsT=xs[0][:, 0, 0:P], rhs=xs[0][:, 0, 0:BANK], start=True, stop=True)
                     for a in range(PASSES):
                         m0 = (a * SIZES[g] + s) * P
                         m_cols = slice(m0, m0 + P)

@@ -24,7 +24,7 @@ SLOTS = 16
 SIZES = [1, 1, 2, 2, 2, 2, 2, 2, 1, 1]
 NG = len(SIZES)
 EPS = 1e-5
-LATE = 2
+LATE = 1
 
 
 def tile_retentivenetwork_pb_kernel(tc, ret, gamma, beta, Wo, bo, out):
@@ -199,9 +199,9 @@ def tile_retentivenetwork_pb_kernel(tc, ret, gamma, beta, Wo, bo, out):
                 for n in range(E // BANK):
                     n_cols = slice(n * BANK, (n + 1) * BANK)
                     nc.vector.tensor_tensor(out=o[:, s, n_cols], in0=acc[(g, s, n)][:], in1=bias_b[:, n_cols], op=ALU.add)
-                    if g == NG - 1:
+                    if g >= NG - 2:
                         nc.sync.dma_start(out=out_v[:, first[g] + s, n_cols], in_=o[:, s, n_cols])
-            if g < NG - 1:
+            if g < NG - 2:
                 nc.sync.dma_start(out=out_v[:, first[g]:first[g] + SIZES[g], :], in_=o[:])
 
         def live(g):

@@ -180,8 +180,6 @@ def tile_retentivenetwork_pb_kernel(tc, ret, gamma, beta, Wo, bo, out):
             for s in range(SIZES[g]):
                 for n in range(E // BANK):
                     acc[(g, s, n)] = apsum.tile([P, BANK], F32, tag="acc", name="acc")
-                    if g >= 5 and s == 0 and n == 0:
-                        nc.tensor.matmul(out=acc[(g, s, n)][:], lhsT=xs[0][:, 0, 0:P], rhs=xs[0][:, 0, 0:BANK], start=True, stop=True)
                     for a in range(PASSES):
                         m0 = (a * SIZES[g] + s) * P
                         m_cols = slice(m0, m0 + P)

from contextlib import ExitStack

import concourse.mybir as mybir
from concourse.masks import make_identity

FLOPS = 2 * 2048 * 1024 * 1024

BF16 = mybir.dt.bfloat16
F32 = mybir.dt.float32
U32 = mybir.dt.uint32
U8 = mybir.dt.uint8
FP8X4 = mybir.dt.float8_e4m3fn_x4
ALU = mybir.AluOpType
ACT = mybir.ActivationFunctionType

P = 128
D = 1024
E = 1024
H = 8
PASSES = 2
PACK = 4
BANK = 512
SLOTS = 16
SIZES = [1, 1, 2, 2, 2, 2, 2, 2, 1, 1]
NG = len(SIZES)
EPS = 1e-5
LATE = 1


def tile_retentivenetwork_pb_kernel(tc, ret, gamma, beta, Wo, bo, out):
    nc = tc.nc
    ret_v = ret.rearrange("b (q j) h c -> (b q) j (h c)", j=SLOTS)
    out_v = out.rearrange("b (q j) e -> (b q) j e", j=SLOTS)
    wo_v = Wo.rearrange("(a p t) n -> p a t n", a=PASSES, t=PACK)
    first = [sum(SIZES[:g]) for g in range(NG)]

    with ExitStack() as ctx:
        const = ctx.enter_context(tc.tile_pool(name="const", bufs=1))
        small = ctx.enter_context(tc.tile_pool(name="small", bufs=NG))
        zpool = ctx.enter_context(tc.tile_pool(name="zpool", bufs=2))
        ppool = ctx.enter_context(tc.tile_pool(name="ppool", bufs=2))
        gpool = ctx.enter_context(tc.tile_pool(name="gpool", bufs=2))
        cpool = ctx.enter_context(tc.tile_pool(name="cpool", bufs=2))
        opool = ctx.enter_context(tc.tile_pool(name="opool", bufs=3))
        tpsum = ctx.enter_context(tc.psum_pool(name="tpsum", bufs=4))
        apsum = ctx.enter_context(tc.psum_pool(name="apsum", bufs=4))
        ctx.enter_context(tc.manual_schedule())

        xs = []
        for g in range(NG):
            xg = const.tile([P, SIZES[g], D], BF16, name="x%d" % g)
            xs.append(xg)
        wraw = const.tile([P, PASSES * PACK, E], BF16, name="wraw")
        bias_b = const.tile([P, E], BF16, name="bias_b")

        def load_x(g):
            nc.sync.dma_start(out=xs[g][:], in_=ret_v[:, first[g]:first[g] + SIZES[g], :])

        def load_w(a):
            nc.sync.dma_start(out=wraw[:, PACK * a:PACK * (a + 1), :], in_=wo_v[:, a, :, :])

        gam = const.tile([P, PASSES, PACK], BF16, name="gam")
        bet = const.tile([P, PASSES, PACK], BF16, name="bet")
        one = const.tile([P, 1], F32, name="one")
        nc.vector.memset(one[:], 1.0)
        nc.scalar.dma_start(out=gam[:], in_=gamma.rearrange("(a p t) -> p a t", a=PASSES, t=PACK))
        nc.scalar.dma_start(out=bet[:], in_=beta.rearrange("(a p t) -> p a t", a=PASSES, t=PACK))
        for h in range(PASSES):
            half = slice(h * BANK, (h + 1) * BANK)
            nc.sync.dma_start(out=xs[0][:, 0, half], in_=ret_v[:, 0, half])
        load_x(1)
        load_x(2)
        load_w(1)
        load_x(3)
        load_w(0)
        for g in range(4, NG):
            load_x(g)
        nc.sync.dma_start(out=bias_b[:], in_=bo.partition_broadcast(P))
        warm = const.tile([P, 1], F32, name="warm")
        nc.scalar.activation(out=warm[:], in_=one[:], func=ACT.Abs_reciprocal_sqrt)

        ident = const.tile([P, P], F32, name="ident")
        make_identity(nc, ident[:])
        gbT = const.tile([P, 2 * H], F32, name="gbT")
        nc.gpsimd.tensor_copy(out=gbT[:, 0:H], in_=gam[:].rearrange("p a t -> p (a t)"))
        nc.gpsimd.tensor_copy(out=gbT[:, H:2 * H], in_=bet[:].rearrange("p a t -> p (a t)"))

        wgrp = const.tile([P, PASSES, E, PACK], BF16, name="wgrp", align_bytes=64)
        wc = const.tile([P, PASSES, E], U32, name="wc", align_bytes=64)
        ws = const.tile([P, PASSES, E], U8, name="ws", align_bytes=64)

        def w_views(a, half):
            cols = slice(half * BANK, (half + 1) * BANK)
            return (wgrp[:, a, cols, :].rearrange("p (c i) t -> p c t i", i=4),
                    wraw[:, PACK * a:PACK * (a + 1), cols].rearrange("p t (c i) -> p c t i", i=4))

        def regroup_w_vector(a, half):
            dst, src = w_views(a, half)
            nc.vector.tensor_copy(out=dst, in_=src)

        def regroup_w_scalar(a, half):
            dst, src = w_views(a, half)
            nc.scalar.copy(out=dst, in_=src)

        def quantise_w(a):
            nc.vector.quantize_mx(
                out=wc[:, a, :].bitcast(FP8X4), scales=ws[:, a, :],
                in_=wgrp[:, a, :, :].rearrange("p c t -> p (c t)"),
            )

        st, rstd, nb, z, zt, yp, yg, yc, ys, acc = {}, {}, {}, {}, {}, {}, {}, {}, {}, {}

        def measure(g, part=2):
            if part != 1:
                st[g] = small.tile([P, SIZES[g] * H, 3], F32, name="st")
            for s in range(SIZES[g]):
                for h in range(0, H, 2):
                    u = s * H + h
                    if part < 2 and u * 2 // (SIZES[g] * H) != part:
                        continue
                    nc.vector.bn_stats(
                        out=st[g][:, u:u + 2, :].rearrange("p u v -> p (u v)"),
                        in_=xs[g][:, s, h * P:(h + 2) * P].rearrange("p (e c) -> p c e", e=2),
                    )

        def root(g):
            rstd[g] = small.tile([P, SIZES[g] * H, 1], F32, name="rstd")
            nc.scalar.activation(out=rstd[g][:], in_=st[g][:, :, 2:3], func=ACT.Abs_reciprocal_sqrt, scale=1.0 / P, bias=EPS)

        def shift(g):
            nb[g] = small.tile([P, SIZES[g] * H, 1], F32, name="nb")
            nc.vector.scalar_tensor_tensor(out=nb[g][:], in0=st[g][:, :, 1:2], scalar=-1.0, in1=rstd[g][:], op0=ALU.mult, op1=ALU.mult)

        def normalise(g, a):
            if a == 0:
                z[g] = zpool.tile([P, SIZES[g], H, P], F32, name="z")
            for j in range(PACK):
                h = PACK * a + j
                for s in range(SIZES[g]):
                    u = s * H + h
                    nc.scalar.activation(
                        out=z[g][:, s, PACK * a:PACK * (a + 1), 32 * j:32 * (j + 1)],
                        in_=xs[g][:, s, h * P:(h + 1) * P].rearrange("p (i t) -> p t i", t=PACK),
                        func=ACT.Identity, bias=nb[g][:, u, :], scale=rstd[g][:, u, :],
                    )

        def turn(g, a):
            for v in range(PACK * a, PACK * (a + 1), 2):
                pair = tpsum.tile([P, 2, BANK // 2], F32, tag="zt", name="zt")
                for i in range(2):
                    zt[(g, v + i)] = pair[:, i, :]
                    for s in range(SIZES[g]):
                        nc.tensor.transpose(out=pair[:, i, s * P:(s + 1) * P], in_=z[g][:, s, v + i, :], identity=ident[:])

        def leave_psum(g, a):
            yp[(g, a)] = ppool.tile([P, PACK, SIZES[g] * P], BF16, name="yp%d" % a)
            for t in (1, 0, 3, 2):
                v = PACK * a + t
                nc.scalar.activation(
                    out=yp[(g, a)][:, t, :], in_=zt[(g, v)][:, 0:SIZES[g] * P], func=ACT.Identity,
                    bias=gbT[:, H + v:H + v + 1], scale=gbT[:, v:v + 1],
                )

        def regroup_y(g, a, go):
            if a == 0:
                yg[g] = gpool.tile([P, PASSES, SIZES[g] * P, PACK], BF16, name="yg", align_bytes=64)
            src = yp[(g, a)][:].rearrange("p t c -> p c t")
            if g >= NG - LATE:
                nc.vector.tensor_copy(out=yg[g][:, a, :, :], in_=src)
            else:
                nc.gpsimd.tensor_scalar(out=yg[g][:, a, :, :], in0=src, scalar1=go[:, 0:1], scalar2=0.0, op0=ALU.mult, op1=ALU.add)

        def quantise_y(g):
            words = PASSES * SIZES[g] * P
            yc[g] = cpool.tile([P, words], U32, name="yc", align_bytes=64)
            ys[g] = cpool.tile([P, words], U8, name="ys", align_bytes=64)
            nc.vector.quantize_mx(out=yc[g][:].bitcast(FP8X4), scales=ys[g][:], in_=yg[g][:].rearrange("p a c t -> p (a c t)"))

        def project(g):
            for s in range(SIZES[g]):
                for n in range(E // BANK):
                    acc[(g, s, n)] = apsum.tile([P, BANK], F32, tag="acc", name="acc")
                    for a in range(PASSES):
                        m0 = (a * SIZES[g] + s) * P
                        m_cols = slice(m0, m0 + P)
                        n_cols = slice(n * BANK, (n + 1) * BANK)
                        nc.tensor.matmul_mx(
                            out=acc[(g, s, n)][:],
                            lhsT=yc[g][:, m_cols].bitcast(FP8X4), lhsT_scale=ys[g][:, m_cols],
                            rhs=wc[:, a, n_cols].bitcast(FP8X4), rhs_scale=ws[:, a, n_cols],
                            start=(a == 0), stop=(a == PASSES - 1),
                        )

        def finish(g):
            o = opool.tile([P, SIZES[g], E], F32, name="o")
            for s in range(SIZES[g]):
                for n in range(E // BANK):
                    n_cols = slice(n * BANK, (n + 1) * BANK)
                    nc.vector.tensor_tensor(out=o[:, s, n_cols], in0=acc[(g, s, n)][:], in1=bias_b[:, n_cols], op=ALU.add)
                    if g >= NG - 2:
                        nc.sync.dma_start(out=out_v[:, first[g] + s, n_cols], in_=o[:, s, n_cols])
            if g < NG - 2:
                nc.sync.dma_start(out=out_v[:, first[g]:first[g] + SIZES[g], :], in_=o[:])

        def live(g):
            return 0 <= g < NG

        go = one
        for k in range(-2, NG + 2):
            due = [0, 1] if k == 3 else [k - 2] if 3 < k else []
            if k == -1:
                root(0)
            if live(k):
                normalise(k, 0)
            if k >= 0 and live(k + 1):
                root(k + 1)
            if -1 <= k < 2:
                measure(k + 2, 0)
                shift(k + 1)
                measure(k + 2, 1)
            else:
                if live(k + 1) and k >= 0:
                    shift(k + 1)
                if live(k + 2):
                    measure(k + 2)
            if k == 0:
                regroup_w_vector(1, 0)
            if k == 1:
                regroup_w_vector(0, 0)
                regroup_w_vector(0, 1)
            if live(k):
                turn(k, 0)
            if live(k - 1):
                leave_psum(k - 1, 1)
            for g in due:
                project(g)
            if live(k):
                normalise(k, 1)
                leave_psum(k, 0)
                turn(k, 1)
            if k == 1:
                regroup_w_scalar(1, 1)
            if k == 2:
                quantise_w(1)
                quantise_w(0)
            if live(k - 1):
                regroup_y(k - 1, 0, go)
                regroup_y(k - 1, 1, go)
            if k >= NG and live(k - 1):
                quantise_y(k - 1)
            for g in due:
                finish(g)
            if live(k - 1) and k < NG:
                quantise_y(k - 1)
            if 2 <= k < NG - 1:
                go = small.tile([P, 1], F32, name="go")
                nc.vector.memset(go[:], 1.0)
